import numpy as np
import ml_dtypes


def mxq(x, axis, fmt="e4m3"):
    dtype, down = {"e4m3": (ml_dtypes.float8_e4m3fn, 7), "e5m2": (ml_dtypes.float8_e5m2, 14)}[fmt]
    v = np.moveaxis(np.asarray(x, np.float32).astype(ml_dtypes.bfloat16).astype(np.float64), axis, -1)
    blocks = v.reshape(v.shape[:-1] + (-1, 32))
    amax = np.abs(blocks).max(-1, keepdims=True)
    byte = np.maximum(np.where(amax > 0, np.frexp(amax)[1] - 1 + 127, 0) - down, 1)
    scale = np.exp2(byte - 127.0)
    codes = (blocks / scale).astype(np.float32).astype(dtype).astype(np.float64)
    return np.moveaxis((codes * scale).reshape(v.shape), -1, axis)


WIDE = False


def mx_kscale(k):
    if not WIDE:
        return np.ones(k)
    levels = np.array([10, -10, 5, -5, 0])
    a = np.random.permutation(np.resize(levels, k // 512 * 4)).reshape(k // 512, 4)
    idx = np.arange(k)
    return np.exp2(a[idx // 512, idx % 128 // 32])


BF16 = ml_dtypes.bfloat16


def bf(x):
    return np.asarray(x, np.float32).astype(BF16)


def f64(x):
    return np.asarray(x).astype(np.float64)


B, H = 1024, 1024


def sigmoid(v):
    return 1.0 / (1.0 + np.exp(-v))


def setup_inputs():
    s = mx_kscale(H)
    w = lambda: bf(np.random.standard_normal((H, H)) * 0.7 / np.sqrt(H) / s[None, :])
    b = lambda: bf(np.random.standard_normal(H) * 0.5)
    return {"inputs": bf(np.random.standard_normal((B, H)) * s),
            "short_term_memory": bf(np.random.standard_normal((B, H)) * s),
            "Wf": w(), "b_f": b(), "Wi": w(), "b_i": b(), "Wg": w(), "b_g": b(), "Wo": w(), "b_o": b()}


def reference(inputs, short_term_memory, Wf, b_f, Wi, b_i, Wg, b_g, Wo, b_o):
    z = f64(inputs) + f64(short_term_memory)
    zq = mxq(z, 1, "e4m3")
    c = sigmoid((zq @ mxq(f64(Wf), 1, "e4m3").T) + f64(b_f))
    c = c + sigmoid((zq @ mxq(f64(Wi), 1, "e4m3").T) + f64(b_i)) * np.tanh((zq @ mxq(f64(Wg), 1, "e4m3").T) + f64(b_g))
    h = np.tanh(c) * sigmoid((zq @ mxq(f64(Wo), 1, "e4m3").T) + f64(b_o))
    return np.stack((c, h))

@@ -1,0 +1,261 @@
+from contextlib import ExitStack
+
+import concourse.mybir as mybir
+from concourse.masks import make_identity
+
+F32 = mybir.dt.float32
+BF16 = mybir.dt.bfloat16
+U32 = mybir.dt.uint32
+U8 = mybir.dt.uint8
+FP8X4 = mybir.dt.float8_e4m3fn_x4
+FUNC = mybir.ActivationFunctionType
+ALU = mybir.AluOpType
+
+P = 128
+BATCH = 1024
+FEAT = 1024
+GATES = 4
+PACK = 4
+K_PASS = P * PACK
+PASSES = FEAT // K_PASS
+N_TILE = 512
+HALVES = BATCH // N_TILE
+HALF_BLOCKS = N_TILE // P
+ROWS = BATCH // P
+FEAT_BLOCKS = FEAT // P
+PSUM_BANKS = 8
+SECOND_HALF_FROM = 2
+
+FLOPS = 2 * BATCH * FEAT * GATES * FEAT
+
+
+def tile_lstmcell_pa_kernel(
+    tc, inputs, short_term_memory, Wf, b_f, Wi, b_i, Wg, b_g, Wo, b_o, out
+):
+    nc = tc.nc
+    weights = (Wi, Wg, Wf, Wo)
+    biases = (b_i, b_g, b_f, b_o)
+    gate_funcs = (FUNC.Sigmoid, FUNC.Tanh, FUNC.Sigmoid, FUNC.Sigmoid)
+
+    x_rows = inputs.rearrange("(p r) k -> p r k", r=ROWS)
+    s_rows = short_term_memory.rearrange("(p r) k -> p r k", r=ROWS)
+    out_rows = out.rearrange("s (p r) h -> s p r h", r=ROWS)
+
+    with ExitStack() as ctx:
+        ctx.enter_context(tc.manual_schedule())
+        const = ctx.enter_context(tc.tile_pool(name="const", bufs=1))
+        resident = ctx.enter_context(tc.tile_pool(name="resident", bufs=1))
+        grouped = ctx.enter_context(tc.tile_pool(name="grouped", bufs=2))
+        work = ctx.enter_context(tc.tile_pool(name="work", bufs=2))
+        stores = ctx.enter_context(tc.tile_pool(name="stores", bufs=4))
+        psum = ctx.enter_context(tc.psum_pool(name="psum", bufs=PSUM_BANKS))
+
+        x_sb = [
+            resident.tile([P, HALF_BLOCKS, FEAT], BF16, name="x_sb%d" % half)
+            for half in range(HALVES)
+        ]
+        s_sb = [
+            resident.tile([P, HALF_BLOCKS, FEAT], BF16, name="s_sb%d" % half)
+            for half in range(HALVES)
+        ]
+        w_sb = [
+            resident.tile([P, GATES, FEAT], BF16, name="w_sb%d" % fb)
+            for fb in range(FEAT_BLOCKS)
+        ]
+        z_grouped = [
+            resident.tile([P, PASSES, N_TILE, PACK], BF16, name="z_grouped%d" % half, align_bytes=64)
+            for half in range(HALVES)
+        ]
+        z_codes = [
+            resident.tile([P, PASSES, N_TILE], U32, name="z_codes%d" % half, align_bytes=64)
+            for half in range(HALVES)
+        ]
+        z_scales = [
+            resident.tile([P, PASSES, N_TILE], U8, name="z_scales%d" % half, align_bytes=64)
+            for half in range(HALVES)
+        ]
+        w_codes = [
+            resident.tile([P, GATES, PASSES, P], U32, name="w_codes%d" % fb, align_bytes=64)
+            for fb in range(FEAT_BLOCKS)
+        ]
+        w_scales = [
+            resident.tile([P, GATES, PASSES, P], U8, name="w_scales%d" % fb, align_bytes=64)
+            for fb in range(FEAT_BLOCKS)
+        ]
+
+        def load_batch_half(half):
+            for first in range(0, HALF_BLOCKS, 2):
+                rows = slice(HALF_BLOCKS * half + first, HALF_BLOCKS * half + first + 2)
+                nc.sync.dma_start(out=x_sb[half][:, first : first + 2, :], in_=x_rows[:, rows, :])
+                nc.sync.dma_start(out=s_sb[half][:, first : first + 2, :], in_=s_rows[:, rows, :])
+
+        def load_weight_block(fb):
+            for gate in range(GATES):
+                nc.sync.dma_start(
+                    out=w_sb[fb][:, gate, :], in_=weights[gate][fb * P : (fb + 1) * P, :]
+                )
+
+        load_batch_half(0)
+        for fb in range(FEAT_BLOCKS // 2):
+            load_weight_block(fb)
+        load_batch_half(1)
+        for fb in range(FEAT_BLOCKS // 2, FEAT_BLOCKS):
+            load_weight_block(fb)
+
+        bias_rows = const.tile([P, P], BF16)
+        nc.vector.memset(bias_rows[:], 0.0)
+        for gate in range(GATES):
+            nc.scalar.dma_start(
+                out=bias_rows[gate * FEAT_BLOCKS : (gate + 1) * FEAT_BLOCKS, :],
+                in_=biases[gate].rearrange("(r c) -> r c", c=P),
+            )
+        warm = const.tile([P, 1], F32)
+        nc.vector.memset(warm[:], 0.0)
+        nc.scalar.activation(out=warm[:], in_=warm[:], func=FUNC.Sigmoid)
+
+        ident_bf = const.tile([P, P], BF16)
+        make_identity(nc, ident_bf[:])
+        ident_f32 = const.tile([P, P], F32)
+        make_identity(nc, ident_f32[:])
+
+        def copy_out(piece, out_ap, in_ap):
+            if piece % 2 == 0:
+                nc.scalar.copy(out=out_ap, in_=in_ap)
+            else:
+                nc.vector.tensor_copy(out=out_ap, in_=in_ap)
+
+        def flip_bias():
+            bias_t = psum.tile([P, P], BF16, tag="bank")
+            nc.tensor.transpose(bias_t[:], bias_rows[:], ident_bf[:])
+            bias_sb = const.tile([P, GATES * FEAT_BLOCKS], F32)
+            nc.vector.tensor_copy(out=bias_sb[:], in_=bias_t[:, 0 : GATES * FEAT_BLOCKS])
+            return bias_sb
+
+        def flip_z_block(half, j):
+            x_pairs = x_sb[half][:, j, :].rearrange("p (w e) -> p e w", e=2)
+            s_pairs = s_sb[half][:, j, :].rearrange("p (w e) -> p e w", e=2)
+            for g in range(PASSES):
+                z_t = psum.tile([P, PACK, P], F32, tag="bank")
+                for t in range(PACK):
+                    u, e = divmod(t, 2)
+                    pairs = slice((2 * g + u) * P, (2 * g + u + 1) * P)
+                    nc.tensor.matmul(
+                        z_t[:, t, :], lhsT=x_pairs[:, e, pairs], rhs=ident_bf[:],
+                        start=True, stop=False,
+                    )
+                    nc.tensor.matmul(
+                        z_t[:, t, :], lhsT=s_pairs[:, e, pairs], rhs=ident_bf[:],
+                        start=False, stop=True,
+                    )
+                copy_out(
+                    g,
+                    z_grouped[half][:, g, j * P : (j + 1) * P, :],
+                    z_t[:].rearrange("p t b -> p b t"),
+                )
+
+        def quantise_z(half):
+            for g in range(PASSES):
+                nc.vector.quantize_mx(
+                    out=z_codes[half][:, g, :].bitcast(FP8X4),
+                    scales=z_scales[half][:, g, :],
+                    in_=z_grouped[half][:, g, :, :].rearrange("p b t -> p (b t)"),
+                )
+
+        def flip_weight_block(fb):
+            w_grouped = grouped.tile([P, GATES, PASSES, P * PACK], BF16, align_bytes=64)
+            for gate in range(GATES):
+                w_words = w_sb[fb][:, gate, :].bitcast(F32)
+                w_t = psum.tile([P, PASSES * 2, P], F32, tag="bank")
+                for plane in range(PASSES * 2):
+                    nc.tensor.transpose(
+                        w_t[:, plane, :], w_words[:, plane * P : (plane + 1) * P], ident_f32[:]
+                    )
+                copy_out(
+                    gate,
+                    w_grouped[:, gate, :, :].bitcast(F32).rearrange("p g (n u) -> p g n u", u=2),
+                    w_t[:].rearrange("p (g u) n -> p g n u", u=2),
+                )
+            return w_grouped
+
+        def quantise_weight_block(fb, w_grouped):
+            nc.vector.quantize_mx(
+                out=w_codes[fb][:].rearrange("p a g n -> p (a g n)").bitcast(FP8X4),
+                scales=w_scales[fb][:].rearrange("p a g n -> p (a g n)"),
+                in_=w_grouped[:].rearrange("p a g c -> p (a g c)"),
+            )
+
+        def gates(half, fb):
+            acted = []
+            for gate in range(GATES):
+                acc = psum.tile([P, N_TILE], F32, tag="bank")
+                for g in range(PASSES):
+                    nc.tensor.matmul_mx(
+                        out=acc[:],
+                        lhsT=w_codes[fb][:, gate, g, :].bitcast(FP8X4),
+                        lhsT_scale=w_scales[fb][:, gate, g, :],
+                        rhs=z_codes[half][:, g, :].bitcast(FP8X4),
+                        rhs_scale=z_scales[half][:, g, :],
+                        start=(g == 0),
+                        stop=(g == PASSES - 1),
+                    )
+                gate_sb = work.tile([P, N_TILE], F32, name="gate%d" % gate)
+                column = gate * FEAT_BLOCKS + fb
+                nc.scalar.activation(
+                    out=gate_sb[:], in_=acc[:], func=gate_funcs[gate],
+                    bias=bias_sb[:, column : column + 1], scale=1.0,
+                )
+                acted.append(gate_sb)
+            i_sb, g_sb, f_sb, o_sb = acted
+            ig_sb = work.tile([P, N_TILE], F32)
+            nc.vector.tensor_tensor(out=ig_sb[:], in0=i_sb[:], in1=g_sb[:], op=ALU.mult)
+            c_sb = work.tile([P, N_TILE], F32)
+            nc.vector.tensor_tensor(out=c_sb[:], in0=f_sb[:], in1=ig_sb[:], op=ALU.add)
+            return half, fb, c_sb, o_sb
+
+        def turn_back(half, fb, c_sb, o_sb):
+            c_t = psum.tile([P, HALF_BLOCKS, P], F32, tag="bank")
+            o_t = psum.tile([P, HALF_BLOCKS, P], F32, tag="bank")
+            for j in range(HALF_BLOCKS):
+                nc.tensor.transpose(c_t[:, j, :], c_sb[:, j * P : (j + 1) * P], ident_f32[:])
+            for j in range(HALF_BLOCKS):
+                nc.tensor.transpose(o_t[:, j, :], o_sb[:, j * P : (j + 1) * P], ident_f32[:])
+            c_out = stores.tile([P, HALF_BLOCKS, P], F32)
+            nc.vector.tensor_copy(out=c_out[:], in_=c_t[:])
+            rows = slice(HALF_BLOCKS * half, HALF_BLOCKS * (half + 1))
+            nc.sync.dma_start(out=out_rows[0, :, rows, fb * P : (fb + 1) * P], in_=c_out[:])
+            return half, fb, c_out, o_t
+
+        def finish(half, fb, c_out, o_t):
+            tanh_c = work.tile([P, HALF_BLOCKS, P], F32)
+            nc.scalar.activation(out=tanh_c[:], in_=c_out[:], func=FUNC.Tanh)
+            h_out = stores.tile([P, HALF_BLOCKS, P], F32)
+            nc.vector.tensor_tensor(out=h_out[:], in0=o_t[:], in1=tanh_c[:], op=ALU.mult)
+            rows = slice(HALF_BLOCKS * half, HALF_BLOCKS * (half + 1))
+            nc.sync.dma_start(out=out_rows[1, :, rows, fb * P : (fb + 1) * P], in_=h_out[:])
+
+        for j in range(HALF_BLOCKS):
+            flip_z_block(0, j)
+        quantise_z(0)
+        bias_sb = flip_bias()
+        flipped = {0: flip_weight_block(0), 1: flip_weight_block(1)}
+        quantise_weight_block(0, flipped[0])
+
+        acted = None
+        turned = None
+        for half in range(HALVES):
+            for fb in range(FEAT_BLOCKS):
+                if turned is not None:
+                    finish(*turned)
+                if half == 0 and fb + 1 < FEAT_BLOCKS:
+                    quantise_weight_block(fb + 1, flipped[fb + 1])
+                if half == 0 and fb == SECOND_HALF_FROM + HALF_BLOCKS:
+                    quantise_z(1)
+                fresh = gates(half, fb)
+                turned = turn_back(*acted) if acted is not None else None
+                acted = fresh
+                if half == 0 and fb + 2 < FEAT_BLOCKS:
+                    flipped[fb + 2] = flip_weight_block(fb + 2)
+                if half == 0 and 0 <= fb - SECOND_HALF_FROM < HALF_BLOCKS:
+                    flip_z_block(1, fb - SECOND_HALF_FROM)
+        finish(*turned)
+        finish(*turn_back(*acted))

@@ -198,7 +198,9 @@ def tile_lstmcell_pa_kernel(
                         start=(g == 0),
                         stop=(g == PASSES - 1),
                     )
-                gate_sb = work.tile([P, N_TILE], F32, name="gate%d" % gate)
+                gate_sb = work.tile(
+                    [P, N_TILE], F32, name="gate%d" % gate, bufs=(3 if gate == GATES - 1 else 2)
+                )
                 column = gate * FEAT_BLOCKS + fb
                 nc.scalar.activation(
                     out=gate_sb[:], in_=acc[:], func=gate_funcs[gate],
@@ -212,20 +214,20 @@ def tile_lstmcell_pa_kernel(
             nc.vector.tensor_tensor(out=c_sb[:], in0=f_sb[:], in1=ig_sb[:], op=ALU.add)
             return half, fb, c_sb, o_sb
 
-        def turn_back(half, fb, c_sb, o_sb):
+        def turn_c(half, fb, c_sb, o_sb):
             c_t = psum.tile([P, HALF_BLOCKS, P], F32, tag="bank")
-            o_t = psum.tile([P, HALF_BLOCKS, P], F32, tag="bank")
             for j in range(HALF_BLOCKS):
                 nc.tensor.transpose(c_t[:, j, :], c_sb[:, j * P : (j + 1) * P], ident_f32[:])
-            for j in range(HALF_BLOCKS):
-                nc.tensor.transpose(o_t[:, j, :], o_sb[:, j * P : (j + 1) * P], ident_f32[:])
             c_out = stores.tile([P, HALF_BLOCKS, P], F32)
             nc.vector.tensor_copy(out=c_out[:], in_=c_t[:])
             rows = slice(HALF_BLOCKS * half, HALF_BLOCKS * (half + 1))
             nc.sync.dma_start(out=out_rows[0, :, rows, fb * P : (fb + 1) * P], in_=c_out[:])
-            return half, fb, c_out, o_t
+            return half, fb, c_out, o_sb
 
-        def finish(half, fb, c_out, o_t):
+        def finish(half, fb, c_out, o_sb):
+            o_t = psum.tile([P, HALF_BLOCKS, P], F32, tag="bank")
+            for j in range(HALF_BLOCKS):
+                nc.tensor.transpose(o_t[:, j, :], o_sb[:, j * P : (j + 1) * P], ident_f32[:])
             tanh_c = work.tile([P, HALF_BLOCKS, P], F32)
             nc.scalar.activation(out=tanh_c[:], in_=c_out[:], func=FUNC.Tanh)
             h_out = stores.tile([P, HALF_BLOCKS, P], F32)
@@ -237,25 +239,26 @@ def tile_lstmcell_pa_kernel(
             flip_z_block(0, j)
         quantise_z(0)
         bias_sb = flip_bias()
-        flipped = {0: flip_weight_block(0), 1: flip_weight_block(1)}
-        quantise_weight_block(0, flipped[0])
+        for fb in range(2):
+            quantise_weight_block(fb, flip_weight_block(fb))
 
         acted = None
         turned = None
         for half in range(HALVES):
             for fb in range(FEAT_BLOCKS):
+                fresh = gates(half, fb)
+                newly_turned = turn_c(*acted) if acted is not None else None
                 if turned is not None:
                     finish(*turned)
-                if half == 0 and fb + 1 < FEAT_BLOCKS:
-                    quantise_weight_block(fb + 1, flipped[fb + 1])
-                if half == 0 and fb == SECOND_HALF_FROM + HALF_BLOCKS:
-                    quantise_z(1)
-                fresh = gates(half, fb)
-                turned = turn_back(*acted) if acted is not None else None
-                acted = fresh
-                if half == 0 and fb + 2 < FEAT_BLOCKS:
-                    flipped[fb + 2] = flip_weight_block(fb + 2)
-                if half == 0 and 0 <= fb - SECOND_HALF_FROM < HALF_BLOCKS:
-                    flip_z_block(1, fb - SECOND_HALF_FROM)
+                acted, turned = fresh, newly_turned
+                if half == 0:
+                    w_grouped = flip_weight_block(fb + 2) if fb + 2 < FEAT_BLOCKS else None
+                    if 0 <= fb - SECOND_HALF_FROM < HALF_BLOCKS:
+                        flip_z_block(1, fb - SECOND_HALF_FROM)
+                    if w_grouped is not None:
+                        quantise_weight_block(fb + 2, w_grouped)
+                    if fb - SECOND_HALF_FROM == HALF_BLOCKS:
+                        quantise_z(1)
+        newly_turned = turn_c(*acted)
         finish(*turned)
-        finish(*turn_back(*acted))
+        finish(*newly_turned)

@@ -45,7 +45,7 @@ def tile_lstmcell_pa_kernel(
         ctx.enter_context(tc.manual_schedule())
         const = ctx.enter_context(tc.tile_pool(name="const", bufs=1))
         resident = ctx.enter_context(tc.tile_pool(name="resident", bufs=1))
-        grouped = ctx.enter_context(tc.tile_pool(name="grouped", bufs=2))
+        grouped = ctx.enter_context(tc.tile_pool(name="grouped", bufs=2 * GATES))
         work = ctx.enter_context(tc.tile_pool(name="work", bufs=2))
         stores = ctx.enter_context(tc.tile_pool(name="stores", bufs=4))
         psum = ctx.enter_context(tc.psum_pool(name="psum", bufs=PSUM_BANKS))
@@ -84,10 +84,9 @@ def tile_lstmcell_pa_kernel(
         ]
 
         def load_batch_half(half):
-            for first in range(0, HALF_BLOCKS, 2):
-                rows = slice(HALF_BLOCKS * half + first, HALF_BLOCKS * half + first + 2)
-                nc.sync.dma_start(out=x_sb[half][:, first : first + 2, :], in_=x_rows[:, rows, :])
-                nc.sync.dma_start(out=s_sb[half][:, first : first + 2, :], in_=s_rows[:, rows, :])
+            for j in range(HALF_BLOCKS):
+                nc.sync.dma_start(out=x_sb[half][:, j, :], in_=x_rows[:, HALF_BLOCKS * half + j, :])
+                nc.sync.dma_start(out=s_sb[half][:, j, :], in_=s_rows[:, HALF_BLOCKS * half + j, :])
 
         def load_weight_block(fb):
             for gate in range(GATES):
@@ -161,27 +160,26 @@ def tile_lstmcell_pa_kernel(
                     in_=z_grouped[half][:, g, :, :].rearrange("p b t -> p (b t)"),
                 )
 
-        def flip_weight_block(fb):
-            w_grouped = grouped.tile([P, GATES, PASSES, P * PACK], BF16, align_bytes=64)
-            for gate in range(GATES):
-                w_words = w_sb[fb][:, gate, :].bitcast(F32)
-                w_t = psum.tile([P, PASSES * 2, P], F32, tag="bank")
-                for plane in range(PASSES * 2):
-                    nc.tensor.transpose(
-                        w_t[:, plane, :], w_words[:, plane * P : (plane + 1) * P], ident_f32[:]
-                    )
-                copy_out(
-                    gate,
-                    w_grouped[:, gate, :, :].bitcast(F32).rearrange("p g (n u) -> p g n u", u=2),
-                    w_t[:].rearrange("p (g u) n -> p g n u", u=2),
+        def flip_weight(fb, gate):
+            w_words = w_sb[fb][:, gate, :].bitcast(F32)
+            w_t = psum.tile([P, PASSES * 2, P], F32, tag="bank")
+            for plane in range(PASSES * 2):
+                nc.tensor.transpose(
+                    w_t[:, plane, :], w_words[:, plane * P : (plane + 1) * P], ident_f32[:]
                 )
+            w_grouped = grouped.tile([P, PASSES, P * PACK], BF16, align_bytes=64)
+            copy_out(
+                gate,
+                w_grouped[:].bitcast(F32).rearrange("p g (n u) -> p g n u", u=2),
+                w_t[:].rearrange("p (g u) n -> p g n u", u=2),
+            )
             return w_grouped
 
-        def quantise_weight_block(fb, w_grouped):
+        def quantise_weight(fb, gate, w_grouped):
             nc.vector.quantize_mx(
-                out=w_codes[fb][:].rearrange("p a g n -> p (a g n)").bitcast(FP8X4),
-                scales=w_scales[fb][:].rearrange("p a g n -> p (a g n)"),
-                in_=w_grouped[:].rearrange("p a g c -> p (a g c)"),
+                out=w_codes[fb][:, gate, :, :].rearrange("p g n -> p (g n)").bitcast(FP8X4),
+                scales=w_scales[fb][:, gate, :, :].rearrange("p g n -> p (g n)"),
+                in_=w_grouped[:].rearrange("p g c -> p (g c)"),
             )
 
         def gates(half, fb):
@@ -239,8 +237,11 @@ def tile_lstmcell_pa_kernel(
             flip_z_block(0, j)
         quantise_z(0)
         bias_sb = flip_bias()
-        for fb in range(2):
-            quantise_weight_block(fb, flip_weight_block(fb))
+        for gate in range(GATES):
+            quantise_weight(0, gate, flip_weight(0, gate))
+        flipped = [flip_weight(1, gate) for gate in range(GATES)]
+        for gate in range(GATES):
+            quantise_weight(1, gate, flipped[gate])
 
         acted = None
         turned = None
@@ -252,11 +253,14 @@ def tile_lstmcell_pa_kernel(
                     finish(*turned)
                 acted, turned = fresh, newly_turned
                 if half == 0:
-                    w_grouped = flip_weight_block(fb + 2) if fb + 2 < FEAT_BLOCKS else None
+                    ahead = fb + 2 if fb + 2 < FEAT_BLOCKS else None
+                    if ahead is not None:
+                        flipped = [flip_weight(ahead, gate) for gate in range(GATES)]
                     if 0 <= fb - SECOND_HALF_FROM < HALF_BLOCKS:
                         flip_z_block(1, fb - SECOND_HALF_FROM)
-                    if w_grouped is not None:
-                        quantise_weight_block(fb + 2, w_grouped)
+                    if ahead is not None:
+                        for gate in range(GATES):
+                            quantise_weight(ahead, gate, flipped[gate])
                     if fb - SECOND_HALF_FROM == HALF_BLOCKS:
                         quantise_z(1)
         newly_turned = turn_c(*acted)

@@ -45,7 +45,7 @@ def tile_lstmcell_pa_kernel(
         ctx.enter_context(tc.manual_schedule())
         const = ctx.enter_context(tc.tile_pool(name="const", bufs=1))
         resident = ctx.enter_context(tc.tile_pool(name="resident", bufs=1))
-        grouped = ctx.enter_context(tc.tile_pool(name="grouped", bufs=2 * GATES))
+        grouped = ctx.enter_context(tc.tile_pool(name="grouped", bufs=2))
         work = ctx.enter_context(tc.tile_pool(name="work", bufs=2))
         stores = ctx.enter_context(tc.tile_pool(name="stores", bufs=4))
         psum = ctx.enter_context(tc.psum_pool(name="psum", bufs=PSUM_BANKS))
@@ -84,9 +84,10 @@ def tile_lstmcell_pa_kernel(
         ]
 
         def load_batch_half(half):
-            for j in range(HALF_BLOCKS):
-                nc.sync.dma_start(out=x_sb[half][:, j, :], in_=x_rows[:, HALF_BLOCKS * half + j, :])
-                nc.sync.dma_start(out=s_sb[half][:, j, :], in_=s_rows[:, HALF_BLOCKS * half + j, :])
+            for first in range(0, HALF_BLOCKS, 2):
+                rows = slice(HALF_BLOCKS * half + first, HALF_BLOCKS * half + first + 2)
+                nc.sync.dma_start(out=x_sb[half][:, first : first + 2, :], in_=x_rows[:, rows, :])
+                nc.sync.dma_start(out=s_sb[half][:, first : first + 2, :], in_=s_rows[:, rows, :])
 
         def load_weight_block(fb):
             for gate in range(GATES):
@@ -160,26 +161,27 @@ def tile_lstmcell_pa_kernel(
                     in_=z_grouped[half][:, g, :, :].rearrange("p b t -> p (b t)"),
                 )
 
-        def flip_weight(fb, gate):
-            w_words = w_sb[fb][:, gate, :].bitcast(F32)
-            w_t = psum.tile([P, PASSES * 2, P], F32, tag="bank")
-            for plane in range(PASSES * 2):
-                nc.tensor.transpose(
-                    w_t[:, plane, :], w_words[:, plane * P : (plane + 1) * P], ident_f32[:]
+        def flip_weight_block(fb):
+            w_grouped = grouped.tile([P, GATES, PASSES, P * PACK], BF16, align_bytes=64)
+            for gate in range(GATES):
+                w_words = w_sb[fb][:, gate, :].bitcast(F32)
+                w_t = psum.tile([P, PASSES * 2, P], F32, tag="bank")
+                for plane in range(PASSES * 2):
+                    nc.tensor.transpose(
+                        w_t[:, plane, :], w_words[:, plane * P : (plane + 1) * P], ident_f32[:]
+                    )
+                copy_out(
+                    gate,
+                    w_grouped[:, gate, :, :].bitcast(F32).rearrange("p g (n u) -> p g n u", u=2),
+                    w_t[:].rearrange("p (g u) n -> p g n u", u=2),
                 )
-            w_grouped = grouped.tile([P, PASSES, P * PACK], BF16, align_bytes=64)
-            copy_out(
-                gate,
-                w_grouped[:].bitcast(F32).rearrange("p g (n u) -> p g n u", u=2),
-                w_t[:].rearrange("p (g u) n -> p g n u", u=2),
-            )
             return w_grouped
 
-        def quantise_weight(fb, gate, w_grouped):
+        def quantise_weight_block(fb, w_grouped):
             nc.vector.quantize_mx(
-                out=w_codes[fb][:, gate, :, :].rearrange("p g n -> p (g n)").bitcast(FP8X4),
-                scales=w_scales[fb][:, gate, :, :].rearrange("p g n -> p (g n)"),
-                in_=w_grouped[:].rearrange("p g c -> p (g c)"),
+                out=w_codes[fb][:].rearrange("p a g n -> p (a g n)").bitcast(FP8X4),
+                scales=w_scales[fb][:].rearrange("p a g n -> p (a g n)"),
+                in_=w_grouped[:].rearrange("p a g c -> p (a g c)"),
             )
 
         def gates(half, fb):
@@ -207,9 +209,9 @@ def tile_lstmcell_pa_kernel(
                 acted.append(gate_sb)
             i_sb, g_sb, f_sb, o_sb = acted
             ig_sb = work.tile([P, N_TILE], F32)
-            nc.vector.tensor_tensor(out=ig_sb[:], in0=i_sb[:], in1=g_sb[:], op=ALU.mult)
+            nc.gpsimd.tensor_tensor(out=ig_sb[:], in0=i_sb[:], in1=g_sb[:], op=ALU.mult)
             c_sb = work.tile([P, N_TILE], F32)
-            nc.vector.tensor_tensor(out=c_sb[:], in0=f_sb[:], in1=ig_sb[:], op=ALU.add)
+            nc.gpsimd.tensor_tensor(out=c_sb[:], in0=f_sb[:], in1=ig_sb[:], op=ALU.add)
             return half, fb, c_sb, o_sb
 
         def turn_c(half, fb, c_sb, o_sb):
@@ -237,11 +239,8 @@ def tile_lstmcell_pa_kernel(
             flip_z_block(0, j)
         quantise_z(0)
         bias_sb = flip_bias()
-        for gate in range(GATES):
-            quantise_weight(0, gate, flip_weight(0, gate))
-        flipped = [flip_weight(1, gate) for gate in range(GATES)]
-        for gate in range(GATES):
-            quantise_weight(1, gate, flipped[gate])
+        for fb in range(2):
+            quantise_weight_block(fb, flip_weight_block(fb))
 
         acted = None
         turned = None
@@ -253,14 +252,11 @@ def tile_lstmcell_pa_kernel(
                     finish(*turned)
                 acted, turned = fresh, newly_turned
                 if half == 0:
-                    ahead = fb + 2 if fb + 2 < FEAT_BLOCKS else None
-                    if ahead is not None:
-                        flipped = [flip_weight(ahead, gate) for gate in range(GATES)]
+                    w_grouped = flip_weight_block(fb + 2) if fb + 2 < FEAT_BLOCKS else None
                     if 0 <= fb - SECOND_HALF_FROM < HALF_BLOCKS:
                         flip_z_block(1, fb - SECOND_HALF_FROM)
-                    if ahead is not None:
-                        for gate in range(GATES):
-                            quantise_weight(ahead, gate, flipped[gate])
+                    if w_grouped is not None:
+                        quantise_weight_block(fb + 2, w_grouped)
                     if fb - SECOND_HALF_FROM == HALF_BLOCKS:
                         quantise_z(1)
         newly_turned = turn_c(*acted)

from contextlib import ExitStack

import concourse.mybir as mybir
from concourse.masks import make_identity

F32 = mybir.dt.float32
BF16 = mybir.dt.bfloat16
U32 = mybir.dt.uint32
U8 = mybir.dt.uint8
FP8X4 = mybir.dt.float8_e4m3fn_x4
FUNC = mybir.ActivationFunctionType
ALU = mybir.AluOpType

P = 128
BATCH = 1024
FEAT = 1024
GATES = 4
PACK = 4
K_PASS = P * PACK
PASSES = FEAT // K_PASS
N_TILE = 512
HALVES = BATCH // N_TILE
HALF_BLOCKS = N_TILE // P
ROWS = BATCH // P
FEAT_BLOCKS = FEAT // P
PSUM_BANKS = 8
SECOND_HALF_FROM = 2

FLOPS = 2 * BATCH * FEAT * GATES * FEAT


def tile_lstmcell_pa_kernel(
    tc, inputs, short_term_memory, Wf, b_f, Wi, b_i, Wg, b_g, Wo, b_o, out
):
    nc = tc.nc
    weights = (Wi, Wg, Wf, Wo)
    biases = (b_i, b_g, b_f, b_o)
    gate_funcs = (FUNC.Sigmoid, FUNC.Tanh, FUNC.Sigmoid, FUNC.Sigmoid)

    x_rows = inputs.rearrange("(p r) k -> p r k", r=ROWS)
    s_rows = short_term_memory.rearrange("(p r) k -> p r k", r=ROWS)
    out_rows = out.rearrange("s (p r) h -> s p r h", r=ROWS)

    with ExitStack() as ctx:
        ctx.enter_context(tc.manual_schedule())
        const = ctx.enter_context(tc.tile_pool(name="const", bufs=1))
        resident = ctx.enter_context(tc.tile_pool(name="resident", bufs=1))
        grouped = ctx.enter_context(tc.tile_pool(name="grouped", bufs=2))
        work = ctx.enter_context(tc.tile_pool(name="work", bufs=2))
        stores = ctx.enter_context(tc.tile_pool(name="stores", bufs=4))
        psum = ctx.enter_context(tc.psum_pool(name="psum", bufs=PSUM_BANKS))

        x_sb = [
            resident.tile([P, HALF_BLOCKS, FEAT], BF16, name="x_sb%d" % half)
            for half in range(HALVES)
        ]
        s_sb = [
            resident.tile([P, HALF_BLOCKS, FEAT], BF16, name="s_sb%d" % half)
            for half in range(HALVES)
        ]
        w_sb = [
            resident.tile([P, GATES, FEAT], BF16, name="w_sb%d" % fb)
            for fb in range(FEAT_BLOCKS)
        ]
        z_grouped = [
            resident.tile([P, PASSES, N_TILE, PACK], BF16, name="z_grouped%d" % half, align_bytes=64)
            for half in range(HALVES)
        ]
        z_codes = [
            resident.tile([P, PASSES, N_TILE], U32, name="z_codes%d" % half, align_bytes=64)
            for half in range(HALVES)
        ]
        z_scales = [
            resident.tile([P, PASSES, N_TILE], U8, name="z_scales%d" % half, align_bytes=64)
            for half in range(HALVES)
        ]
        w_codes = [
            resident.tile([P, GATES, PASSES, P], U32, name="w_codes%d" % fb, align_bytes=64)
            for fb in range(FEAT_BLOCKS)
        ]
        w_scales = [
            resident.tile([P, GATES, PASSES, P], U8, name="w_scales%d" % fb, align_bytes=64)
            for fb in range(FEAT_BLOCKS)
        ]

        def load_batch_half(half):
            for first in range(0, HALF_BLOCKS, 2):
                rows = slice(HALF_BLOCKS * half + first, HALF_BLOCKS * half + first + 2)
                nc.sync.dma_start(out=x_sb[half][:, first : first + 2, :], in_=x_rows[:, rows, :])
                nc.sync.dma_start(out=s_sb[half][:, first : first + 2, :], in_=s_rows[:, rows, :])

        def load_weight_block(fb):
            for gate in range(GATES):
                nc.sync.dma_start(
                    out=w_sb[fb][:, gate, :], in_=weights[gate][fb * P : (fb + 1) * P, :]
                )

        load_batch_half(0)
        for fb in range(FEAT_BLOCKS // 2):
            load_weight_block(fb)
        load_batch_half(1)
        for fb in range(FEAT_BLOCKS // 2, FEAT_BLOCKS):
            load_weight_block(fb)

        bias_rows = const.tile([P, P], BF16)
        nc.vector.memset(bias_rows[:], 0.0)
        for gate in range(GATES):
            nc.scalar.dma_start(
                out=bias_rows[gate * FEAT_BLOCKS : (gate + 1) * FEAT_BLOCKS, :],
                in_=biases[gate].rearrange("(r c) -> r c", c=P),
            )
        warm = const.tile([P, 1], F32)
        nc.vector.memset(warm[:], 0.0)
        nc.scalar.activation(out=warm[:], in_=warm[:], func=FUNC.Sigmoid)

        ident_bf = const.tile([P, P], BF16)
        make_identity(nc, ident_bf[:])
        ident_f32 = const.tile([P, P], F32)
        make_identity(nc, ident_f32[:])

        def copy_out(piece, out_ap, in_ap):
            if piece % 2 == 0:
                nc.scalar.copy(out=out_ap, in_=in_ap)
            else:
                nc.vector.tensor_copy(out=out_ap, in_=in_ap)

        def flip_bias():
            bias_t = psum.tile([P, P], BF16, tag="bank")
            nc.tensor.transpose(bias_t[:], bias_rows[:], ident_bf[:])
            bias_sb = const.tile([P, GATES * FEAT_BLOCKS], F32)
            nc.vector.tensor_copy(out=bias_sb[:], in_=bias_t[:, 0 : GATES * FEAT_BLOCKS])
            return bias_sb

        def flip_z_block(half, j):
            x_pairs = x_sb[half][:, j, :].rearrange("p (w e) -> p e w", e=2)
            s_pairs = s_sb[half][:, j, :].rearrange("p (w e) -> p e w", e=2)
            for g in range(PASSES):
                z_t = psum.tile([P, PACK, P], F32, tag="bank")
                for t in range(PACK):
                    u, e = divmod(t, 2)
                    pairs = slice((2 * g + u) * P, (2 * g + u + 1) * P)
                    nc.tensor.matmul(
                        z_t[:, t, :], lhsT=x_pairs[:, e, pairs], rhs=ident_bf[:],
                        start=True, stop=False,
                    )
                    nc.tensor.matmul(
                        z_t[:, t, :], lhsT=s_pairs[:, e, pairs], rhs=ident_bf[:],
                        start=False, stop=True,
                    )
                copy_out(
                    g,
                    z_grouped[half][:, g, j * P : (j + 1) * P, :],
                    z_t[:].rearrange("p t b -> p b t"),
                )

        def quantise_z(half):
            for g in range(PASSES):
                nc.vector.quantize_mx(
                    out=z_codes[half][:, g, :].bitcast(FP8X4),
                    scales=z_scales[half][:, g, :],
                    in_=z_grouped[half][:, g, :, :].rearrange("p b t -> p (b t)"),
                )

        def flip_weight_block(fb):
            w_grouped = grouped.tile([P, GATES, PASSES, P * PACK], BF16, align_bytes=64)
            for gate in range(GATES):
                w_words = w_sb[fb][:, gate, :].bitcast(F32)
                w_t = psum.tile([P, PASSES * 2, P], F32, tag="bank")
                for plane in range(PASSES * 2):
                    nc.tensor.transpose(
                        w_t[:, plane, :], w_words[:, plane * P : (plane + 1) * P], ident_f32[:]
                    )
                copy_out(
                    gate,
                    w_grouped[:, gate, :, :].bitcast(F32).rearrange("p g (n u) -> p g n u", u=2),
                    w_t[:].rearrange("p (g u) n -> p g n u", u=2),
                )
            return w_grouped

        def quantise_weight_block(fb, w_grouped):
            nc.vector.quantize_mx(
                out=w_codes[fb][:].rearrange("p a g n -> p (a g n)").bitcast(FP8X4),
                scales=w_scales[fb][:].rearrange("p a g n -> p (a g n)"),
                in_=w_grouped[:].rearrange("p a g c -> p (a g c)"),
            )

        def gates(half, fb):
            acted = []
            for gate in range(GATES):
                acc = psum.tile([P, N_TILE], F32, tag="bank")
                for g in range(PASSES):
                    nc.tensor.matmul_mx(
                        out=acc[:],
                        lhsT=w_codes[fb][:, gate, g, :].bitcast(FP8X4),
                        lhsT_scale=w_scales[fb][:, gate, g, :],
                        rhs=z_codes[half][:, g, :].bitcast(FP8X4),
                        rhs_scale=z_scales[half][:, g, :],
                        start=(g == 0),
                        stop=(g == PASSES - 1),
                    )
                gate_sb = work.tile(
                    [P, N_TILE], F32, name="gate%d" % gate, bufs=(3 if gate == GATES - 1 else 2)
                )
                column = gate * FEAT_BLOCKS + fb
                nc.scalar.activation(
                    out=gate_sb[:], in_=acc[:], func=gate_funcs[gate],
                    bias=bias_sb[:, column : column + 1], scale=1.0,
                )
                acted.append(gate_sb)
            i_sb, g_sb, f_sb, o_sb = acted
            ig_sb = work.tile([P, N_TILE], F32)
            nc.gpsimd.tensor_tensor(out=ig_sb[:], in0=i_sb[:], in1=g_sb[:], op=ALU.mult)
            c_sb = work.tile([P, N_TILE], F32)
            nc.gpsimd.tensor_tensor(out=c_sb[:], in0=f_sb[:], in1=ig_sb[:], op=ALU.add)
            return half, fb, c_sb, o_sb

        def turn_c(half, fb, c_sb, o_sb):
            c_t = psum.tile([P, HALF_BLOCKS, P], F32, tag="bank")
            for j in range(HALF_BLOCKS):
                nc.tensor.transpose(c_t[:, j, :], c_sb[:, j * P : (j + 1) * P], ident_f32[:])
            c_out = stores.tile([P, HALF_BLOCKS, P], F32)
            nc.vector.tensor_copy(out=c_out[:], in_=c_t[:])
            rows = slice(HALF_BLOCKS * half, HALF_BLOCKS * (half + 1))
            nc.sync.dma_start(out=out_rows[0, :, rows, fb * P : (fb + 1) * P], in_=c_out[:])
            return half, fb, c_out, o_sb

        def finish(half, fb, c_out, o_sb):
            o_t = psum.tile([P, HALF_BLOCKS, P], F32, tag="bank")
            for j in range(HALF_BLOCKS):
                nc.tensor.transpose(o_t[:, j, :], o_sb[:, j * P : (j + 1) * P], ident_f32[:])
            tanh_c = work.tile([P, HALF_BLOCKS, P], F32)
            nc.scalar.activation(out=tanh_c[:], in_=c_out[:], func=FUNC.Tanh)
            h_out = stores.tile([P, HALF_BLOCKS, P], F32)
            nc.vector.tensor_tensor(out=h_out[:], in0=o_t[:], in1=tanh_c[:], op=ALU.mult)
            rows = slice(HALF_BLOCKS * half, HALF_BLOCKS * (half + 1))
            nc.sync.dma_start(out=out_rows[1, :, rows, fb * P : (fb + 1) * P], in_=h_out[:])

        for j in range(HALF_BLOCKS):
            flip_z_block(0, j)
        quantise_z(0)
        bias_sb = flip_bias()
        for fb in range(2):
            quantise_weight_block(fb, flip_weight_block(fb))

        acted = None
        turned = None
        for half in range(HALVES):
            for fb in range(FEAT_BLOCKS):
                fresh = gates(half, fb)
                newly_turned = turn_c(*acted) if acted is not None else None
                if turned is not None:
                    finish(*turned)
                acted, turned = fresh, newly_turned
                if half == 0:
                    w_grouped = flip_weight_block(fb + 2) if fb + 2 < FEAT_BLOCKS else None
                    if 0 <= fb - SECOND_HALF_FROM < HALF_BLOCKS:
                        flip_z_block(1, fb - SECOND_HALF_FROM)
                    if w_grouped is not None:
                        quantise_weight_block(fb + 2, w_grouped)
                    if fb - SECOND_HALF_FROM == HALF_BLOCKS:
                        quantise_z(1)
        newly_turned = turn_c(*acted)
        finish(*turned)
        finish(*newly_turned)
